import numpy as np
import ml_dtypes


def mxq(x, axis, fmt="e4m3"):
    dtype, down = {"e4m3": (ml_dtypes.float8_e4m3fn, 7), "e5m2": (ml_dtypes.float8_e5m2, 14)}[fmt]
    v = np.moveaxis(np.asarray(x, np.float32).astype(ml_dtypes.bfloat16).astype(np.float64), axis, -1)
    blocks = v.reshape(v.shape[:-1] + (-1, 32))
    amax = np.abs(blocks).max(-1, keepdims=True)
    byte = np.maximum(np.where(amax > 0, np.frexp(amax)[1] - 1 + 127, 0) - down, 1)
    scale = np.exp2(byte - 127.0)
    codes = (blocks / scale).astype(np.float32).astype(dtype).astype(np.float64)
    return np.moveaxis((codes * scale).reshape(v.shape), -1, axis)


WIDE = False


def mx_kscale(k):
    if not WIDE:
        return np.ones(k)
    levels = np.array([10, -10, 5, -5, 0])
    a = np.random.permutation(np.resize(levels, k // 512 * 4)).reshape(k // 512, 4)
    idx = np.arange(k)
    return np.exp2(a[idx // 512, idx % 128 // 32])


BF16 = ml_dtypes.bfloat16


def bf(x):
    return np.asarray(x, np.float32).astype(BF16)


def f64(x):
    return np.asarray(x).astype(np.float64)


B, D, H, F, K = 2048, 1024, 1024, 1024, 128
EPS_LN = 1e-5


def silu(v):
    return v / (1.0 + np.exp(-v))


def setup_inputs():
    s = mx_kscale(D)
    return {"x": bf(np.random.standard_normal((B, D)) * s),
            "W1": bf(np.random.standard_normal((D, H)) / np.sqrt(D) / s[:, None]),
            "b1": bf(0.2 * np.random.standard_normal(H)),
            "g": bf(1.0 + 0.1 * np.random.standard_normal(H)),
            "beta": bf(0.1 * np.random.standard_normal(H))}


def reference(x, W1, b1, g, beta):
    h = silu((mxq(f64(x), 1, "e4m3") @ mxq(f64(W1), 0, "e4m3")) + f64(b1))
    mu = h.mean(-1, keepdims=True)
    var = ((h - mu) ** 2).mean(-1, keepdims=True)
    return (h - mu) / np.sqrt(var + EPS_LN) * f64(g) + f64(beta)

@@ -1,0 +1,261 @@
+from contextlib import ExitStack
+
+import concourse.mybir as mybir
+from concourse.masks import make_identity
+
+F32 = mybir.dt.float32
+BF16 = mybir.dt.bfloat16
+U32 = mybir.dt.uint32
+U8 = mybir.dt.uint8
+I32 = mybir.dt.int32
+FP8X4 = mybir.dt.float8_e4m3fn_x4
+ACT = mybir.ActivationFunctionType
+ALU = mybir.AluOpType
+
+P = 128
+B, D, H = 2048, 1024, 1024
+EPS = 1e-5
+FLOPS = 2 * B * D * H
+NT = B // P
+NJ = H // P
+
+CHUNKS = [2, 2, 4, 4, 4]
+XEXIT = "SSSSVVVVVVSSSSSS"
+STATS = "VVSVSVSVSVSSSVSS"
+XPLAN = [[0, 1, 2, 3], [4, 5, 6, 7], [8, 9, 10, 11], [12, 13, 14, 15], [], [], [], [], []]
+WV = 336
+PIN = True
+
+
+def tile_evidentialhead_pa_kernel(tc, x, W1, b1, g, beta, out):
+    nc = tc.nc
+    starts = [sum(CHUNKS[:c]) for c in range(len(CHUNKS))]
+    chunk_of = [max(k for k in range(len(CHUNKS)) if starts[k] <= i) for i in range(NT)]
+    with ExitStack() as ctx:
+        const = ctx.enter_context(tc.tile_pool(name="const", bufs=1))
+        wpool = ctx.enter_context(tc.tile_pool(name="wpool", bufs=1))
+        xpool = ctx.enter_context(tc.tile_pool(name="xpool", bufs=1))
+        work = ctx.enter_context(tc.tile_pool(name="work", bufs=2))
+        small = ctx.enter_context(tc.tile_pool(name="small", bufs=6))
+        psum = ctx.enter_context(tc.psum_pool(name="psum", bufs=2))
+        if PIN:
+            ctx.enter_context(tc.manual_schedule())
+
+        rows = const.tile([P, 2 * H + P], BF16, name="rows")
+        nc.vector.memset(rows[:].bitcast(I32), 0)
+        ones = const.tile([P, P], BF16, name="ones")
+        nc.vector.memset(ones[:], 1.0)
+        neg_half = const.tile([P, 1], F32, name="neg_half")
+        nc.vector.memset(neg_half[:], -0.5)
+        ident = const.tile([P, P], F32, name="ident")
+        make_identity(nc, ident[:])
+        nc.scalar.dma_start(out=rows[0:1, 0:H], in_=g.unsqueeze(0))
+        nc.scalar.dma_start(out=rows[0:1, H : 2 * H], in_=beta.unsqueeze(0))
+        nc.scalar.dma_start(out=rows[0:NJ, 2 * H : 2 * H + P], in_=b1.rearrange("(j m) -> j m", m=P))
+
+        wraw = wpool.tile([P, 8, H], BF16, name="wraw")
+        for w in range(4):
+            nc.sync.dma_start(
+                out=wraw[:, 2 * w : 2 * w + 2, :],
+                in_=W1[256 * w : 256 * w + 256, :].rearrange("(p e) c -> p e c", e=2),
+            )
+        xr = []
+        for i in range(NT):
+            xi = xpool.tile([P, D], BF16, name="x%d" % i)
+            nc.sync.dma_start(out=xi[:], in_=x[P * i : P * i + P, :])
+            xr.append(xi)
+
+        gb = const.tile([P, 2 * H], F32, name="gb")
+        for n in range(4):
+            bc = psum.tile([P, 512], F32, name="bc", tag="ps", bufs=6)
+            nc.tensor.matmul(out=bc[:], lhsT=ones[:], rhs=rows[:, 512 * n : 512 * n + 512], start=True, stop=True)
+            if n % 2 == 0:
+                nc.vector.tensor_copy(out=gb[:, 512 * n : 512 * n + 512], in_=bc[:])
+            else:
+                nc.scalar.copy(out=gb[:, 512 * n : 512 * n + 512], in_=bc[:])
+        b1f = const.tile([P, P], F32, name="b1f")
+        nc.vector.tensor_copy(out=b1f[:], in_=rows[:, 2 * H : 2 * H + P])
+        b1p = psum.tile([P, 4, P], F32, name="b1p", tag="ps", bufs=6)
+        nc.tensor.transpose(b1p[:, 0, :], b1f[:], ident[:])
+        b1T = const.tile([P, NJ], F32, name="b1T")
+        nc.vector.tensor_copy(out=b1T[:], in_=b1p[:, 0, 0:NJ])
+
+        wg = wpool.tile([P, 2, H, 4], BF16, name="wg", align_bytes=64)
+        wq = wpool.tile([P, 2, H], U32, name="wq", align_bytes=64)
+        ws = wpool.tile([P, 2, H], U8, name="ws", align_bytes=64)
+
+        def w_regroup(gi, h):
+            for eng, lo, hi in (("V", 512 * h, 512 * h + WV), ("S", 512 * h + WV, 512 * h + 512)):
+                dst = wg[:, gi, lo:hi, :].rearrange("p (c i) t -> p c t i", i=4)
+                src = wraw[:, 4 * gi : 4 * gi + 4, lo:hi].rearrange("p t (c i) -> p c t i", i=4)
+                if eng == "V":
+                    nc.vector.tensor_copy(out=dst, in_=src)
+                else:
+                    nc.scalar.copy(out=dst, in_=src)
+
+        def w_quant(gi, h):
+            cols = slice(512 * h, 512 * h + 512)
+            nc.vector.quantize_mx(
+                out=wq[:, gi, cols].bitcast(FP8X4),
+                scales=ws[:, gi, cols],
+                in_=wg[:, gi, cols, :].rearrange("p c t -> p (c t)"),
+            )
+
+        xg = {}
+        xq = {}
+        xs = {}
+
+        def x_prep(i):
+            c = chunk_of[i]
+            r = i - starts[c]
+            nb = P * CHUNKS[c]
+            if r == 0:
+                xg[c] = work.tile([P, 8 * nb], BF16, name="xg", tag="xg", bufs=2, align_bytes=64)
+            xt = psum.tile([P, 4, P], F32, name="xt", tag="ps", bufs=6)
+            xw = xr[i][:].bitcast(F32)
+            for w in range(4):
+                nc.tensor.transpose(xt[:, w, :], xw[:, P * w : P * w + P], ident[:])
+            dst = xg[c][:].bitcast(F32).rearrange("p (g b u) -> p g b u", g=2, u=2)[:, :, P * r : P * r + P, :]
+            src = xt[:].rearrange("p (g u) b -> p g b u", g=2)
+            if XEXIT[i] == "V":
+                nc.vector.tensor_copy(out=dst, in_=src)
+            else:
+                nc.scalar.copy(out=dst, in_=src)
+
+        def x_quant(c):
+            nb = P * CHUNKS[c]
+            xq[c] = xpool.tile([P, 2 * nb], U32, name="xq%d" % c, align_bytes=64)
+            xs[c] = xpool.tile([P, 2 * nb], U8, name="xs%d" % c, align_bytes=64)
+            nc.vector.quantize_mx(out=xq[c][:].bitcast(FP8X4), scales=xs[c][:], in_=xg[c][:])
+
+        hT = {}
+
+        def mx_group(c, j):
+            nb = P * CHUNKS[c]
+            if j == 0:
+                hT[c] = work.tile([P, NJ, nb], F32, name="hT", tag="hT", bufs=2)
+            acc = psum.tile([P, 512], F32, name="acc", tag="acc")
+            for gi in range(2):
+                nc.tensor.matmul_mx(
+                    out=acc[:, 0:nb],
+                    lhsT=wq[:, gi, P * j : P * j + P].bitcast(FP8X4),
+                    lhsT_scale=ws[:, gi, P * j : P * j + P],
+                    rhs=xq[c][:, nb * gi : nb * gi + nb].bitcast(FP8X4),
+                    rhs_scale=xs[c][:, nb * gi : nb * gi + nb],
+                    start=(gi == 0),
+                    stop=(gi == 1),
+                )
+            nc.scalar.activation(out=hT[c][:, j, :], in_=acc[:, 0:nb], func=ACT.Silu, bias=b1T[:, j : j + 1], scale=1.0)
+
+        junk = const.tile([P, 512], F32, name="junk")
+        hA = {}
+        shift = {}
+        rstd = {}
+        tt = {}
+
+        def back(i):
+            c = chunk_of[i]
+            r = i - starts[c]
+            hA[i] = []
+            for a in range(2):
+                ha = psum.tile([P, 512], F32, name="hA", tag="ps", bufs=6)
+                for jj in range(4):
+                    nc.tensor.transpose(ha[:, P * jj : P * jj + P], hT[c][:, 4 * a + jj, P * r : P * r + P], ident[:])
+                hA[i].append(ha)
+
+        def stats(i):
+            ve = small.tile([P, 1], F32, name="ve")
+            rstd[i] = small.tile([P, 1], F32, name="rs")
+            if STATS[i] == "V":
+                st = small.tile([P, 2, 6], F32, name="st")
+                for a in range(2):
+                    nc.vector.bn_stats(out=st[:, a, :], in_=hA[i][a][:])
+                mv = small.tile([P, 2], F32, name="mv")
+                nc.vector.bn_aggr(out=mv[:], in_=st[:].rearrange("p a s -> p (a s)"))
+                nc.gpsimd.tensor_scalar(out=ve[:], in0=mv[:, 1:2], scalar1=1.0, scalar2=EPS, op0=ALU.mult, op1=ALU.add)
+                shift[i] = (mv[:, 0:1], ALU.subtract)
+            else:
+                sums = small.tile([P, 2], F32, name="sums")
+                for a in range(2):
+                    nc.scalar.activation(out=junk[:], in_=hA[i][a][:], func=ACT.Identity, accum_out=sums[:, a : a + 1])
+                nm = small.tile([P, 1], F32, name="nm")
+                tmp = small.tile([P, 2], F32, name="tmp")
+                nc.scalar.activation(out=tmp[:], in_=sums[:], func=ACT.Identity, scale=-1.0 / H, accum_out=nm[:])
+                ss = small.tile([P, 2], F32, name="ss")
+                for a in range(2):
+                    nc.scalar.activation(out=junk[:], in_=hA[i][a][:], func=ACT.Square, bias=nm[:], accum_out=ss[:, a : a + 1])
+                var = small.tile([P, 1], F32, name="var")
+                tmp2 = small.tile([P, 2], F32, name="tmp2")
+                nc.scalar.activation(out=tmp2[:], in_=ss[:], func=ACT.Identity, scale=1.0 / H, accum_out=var[:])
+                nm2 = small.tile([P, 1], F32, name="nm2")
+                nc.scalar.copy(out=nm2[:], in_=nm[:])
+                nc.gpsimd.tensor_scalar(out=ve[:], in0=var[:], scalar1=1.0, scalar2=EPS, op0=ALU.mult, op1=ALU.add)
+                shift[i] = (nm2[:], ALU.add)
+            nc.gpsimd.tensor_tensor(out=rstd[i][:], in0=ve[:], in1=neg_half[:], op=ALU.pow)
+
+        def centre(i):
+            tt[i] = work.tile([P, H], F32, name="t", tag="t", bufs=5)
+            for a in range(2):
+                nc.vector.scalar_tensor_tensor(
+                    out=tt[i][:, 512 * a : 512 * a + 512],
+                    in0=hA[i][a][:],
+                    scalar=shift[i][0],
+                    in1=gb[:, 512 * a : 512 * a + 512],
+                    op0=shift[i][1],
+                    op1=ALU.mult,
+                )
+
+        def finish(i):
+            o = work.tile([P, H], F32, name="o", tag="o", bufs=4)
+            nc.vector.scalar_tensor_tensor(
+                out=o[:], in0=tt[i][:], scalar=rstd[i][:], in1=gb[:, H : 2 * H], op0=ALU.mult, op1=ALU.add
+            )
+            nc.sync.dma_start(out=out[P * i : P * i + P, :], in_=o[:])
+
+        def x_plan(tiles):
+            for i in tiles:
+                x_prep(i)
+                c = chunk_of[i]
+                if i == starts[c] + CHUNKS[c] - 1:
+                    x_quant(c)
+
+        w_regroup(0, 0)
+        w_regroup(0, 1)
+        w_quant(0, 0)
+        w_regroup(1, 0)
+        w_quant(0, 1)
+        w_regroup(1, 1)
+        w_quant(1, 0)
+        x_prep(0)
+        x_prep(1)
+        w_quant(1, 1)
+        x_quant(0)
+        x_plan(XPLAN[0][2:])
+        for j in range(NJ):
+            mx_group(0, j)
+        for k in range(NT // 2):
+            pair = [2 * k, 2 * k + 1]
+            c = chunk_of[pair[0]]
+            n = CHUNKS[c] // 2
+            r = (pair[0] - starts[c]) // 2
+            for i in pair:
+                back(i)
+            for i in pair:
+                if STATS[i] == "S":
+                    stats(i)
+            if c + 1 < len(CHUNKS):
+                for j in range(NJ * r // n, NJ * (r + 1) // n):
+                    mx_group(c + 1, j)
+            for i in pair:
+                if STATS[i] == "V":
+                    stats(i)
+                    centre(i)
+            if k > 0:
+                finish(pair[0] - 2)
+                finish(pair[1] - 2)
+            for i in pair:
+                if STATS[i] == "S":
+                    centre(i)
+            x_plan(XPLAN[k + 1])
+        finish(NT - 2)
+        finish(NT - 1)

@@ -20,9 +20,10 @@ NT = B // P
 NJ = H // P
 
 CHUNKS = [2, 2, 4, 4, 4]
-XEXIT = "SSSSVVVVVVSSSSSS"
-STATS = "VVSVSVSVSVSSSVSS"
-XPLAN = [[0, 1, 2, 3], [4, 5, 6, 7], [8, 9, 10, 11], [12, 13, 14, 15], [], [], [], [], []]
+XEXIT = "SSSSVVVVSSSSSSSS"
+STATS = "VVSVSSSVSSSVSSSS"
+ACC = 4
+SHARE = [0, 8, 4, 4, 4, 4, 0, 0]
 WV = 336
 PIN = True
 
@@ -60,14 +61,17 @@ def tile_evidentialhead_pa_kernel(tc, x, W1, b1, g, beta, out):
                 in_=W1[256 * w : 256 * w + 256, :].rearrange("(p e) c -> p e c", e=2),
             )
         xr = []
-        for i in range(NT):
-            xi = xpool.tile([P, D], BF16, name="x%d" % i)
-            nc.sync.dma_start(out=xi[:], in_=x[P * i : P * i + P, :])
-            xr.append(xi)
+        for c in range(len(CHUNKS)):
+            n = CHUNKS[c]
+            xc = xpool.tile([P, n, D], BF16, name="x%d" % c)
+            nc.sync.dma_start(
+                out=xc[:], in_=x[P * starts[c] : P * (starts[c] + n), :].rearrange("(p r) k -> p r k", r=n)
+            )
+            xr.append(xc)
 
         gb = const.tile([P, 2 * H], F32, name="gb")
         for n in range(4):
-            bc = psum.tile([P, 512], F32, name="bc", tag="ps", bufs=6)
+            bc = psum.tile([P, 512], F32, name="bc", tag="acc", bufs=ACC)
             nc.tensor.matmul(out=bc[:], lhsT=ones[:], rhs=rows[:, 512 * n : 512 * n + 512], start=True, stop=True)
             if n % 2 == 0:
                 nc.vector.tensor_copy(out=gb[:, 512 * n : 512 * n + 512], in_=bc[:])
@@ -75,7 +79,7 @@ def tile_evidentialhead_pa_kernel(tc, x, W1, b1, g, beta, out):
                 nc.scalar.copy(out=gb[:, 512 * n : 512 * n + 512], in_=bc[:])
         b1f = const.tile([P, P], F32, name="b1f")
         nc.vector.tensor_copy(out=b1f[:], in_=rows[:, 2 * H : 2 * H + P])
-        b1p = psum.tile([P, 4, P], F32, name="b1p", tag="ps", bufs=6)
+        b1p = psum.tile([P, 4, P], F32, name="b1p", tag="acc", bufs=ACC)
         nc.tensor.transpose(b1p[:, 0, :], b1f[:], ident[:])
         b1T = const.tile([P, NJ], F32, name="b1T")
         nc.vector.tensor_copy(out=b1T[:], in_=b1p[:, 0, 0:NJ])
@@ -105,18 +109,25 @@ def tile_evidentialhead_pa_kernel(tc, x, W1, b1, g, beta, out):
         xq = {}
         xs = {}
 
-        def x_prep(i):
+        xts = {}
+
+        def x_turn(i):
             c = chunk_of[i]
             r = i - starts[c]
             nb = P * CHUNKS[c]
             if r == 0:
                 xg[c] = work.tile([P, 8 * nb], BF16, name="xg", tag="xg", bufs=2, align_bytes=64)
-            xt = psum.tile([P, 4, P], F32, name="xt", tag="ps", bufs=6)
-            xw = xr[i][:].bitcast(F32)
+            xt = psum.tile([P, 4, P], F32, name="xt", tag=("h%d" % (i % 2) if XEXIT[i] == "V" else "acc"), bufs=(2 if XEXIT[i] == "V" else ACC))
+            xw = xr[c][:, r, :].bitcast(F32)
             for w in range(4):
                 nc.tensor.transpose(xt[:, w, :], xw[:, P * w : P * w + P], ident[:])
+            xts[i] = xt
+
+        def x_exit(i):
+            c = chunk_of[i]
+            r = i - starts[c]
             dst = xg[c][:].bitcast(F32).rearrange("p (g b u) -> p g b u", g=2, u=2)[:, :, P * r : P * r + P, :]
-            src = xt[:].rearrange("p (g u) b -> p g b u", g=2)
+            src = xts[i][:].rearrange("p (g u) b -> p g b u", g=2)
             if XEXIT[i] == "V":
                 nc.vector.tensor_copy(out=dst, in_=src)
             else:
@@ -129,12 +140,13 @@ def tile_evidentialhead_pa_kernel(tc, x, W1, b1, g, beta, out):
             nc.vector.quantize_mx(out=xq[c][:].bitcast(FP8X4), scales=xs[c][:], in_=xg[c][:])
 
         hT = {}
+        accs = {}
 
-        def mx_group(c, j):
+        def mx(c, j):
             nb = P * CHUNKS[c]
             if j == 0:
-                hT[c] = work.tile([P, NJ, nb], F32, name="hT", tag="hT", bufs=2)
-            acc = psum.tile([P, 512], F32, name="acc", tag="acc")
+                hT[c] = work.tile([P, NJ, nb], F32, name="hT", tag="hT", bufs=3)
+            acc = psum.tile([P, 512], F32, name="acc", tag="acc", bufs=ACC)
             for gi in range(2):
                 nc.tensor.matmul_mx(
                     out=acc[:, 0:nb],
@@ -145,79 +157,141 @@ def tile_evidentialhead_pa_kernel(tc, x, W1, b1, g, beta, out):
                     start=(gi == 0),
                     stop=(gi == 1),
                 )
-            nc.scalar.activation(out=hT[c][:, j, :], in_=acc[:, 0:nb], func=ACT.Silu, bias=b1T[:, j : j + 1], scale=1.0)
+            accs[(c, j)] = acc
 
-        junk = const.tile([P, 512], F32, name="junk")
+        def silu(c, j):
+            nb = P * CHUNKS[c]
+            nc.scalar.activation(
+                out=hT[c][:, j, :], in_=accs[(c, j)][:, 0:nb], func=ACT.Silu, bias=b1T[:, j : j + 1], scale=1.0
+            )
+
+        junk = const.tile([P, H], F32, name="junk")
+        eps_col = const.tile([P, 1], F32, name="eps_col")
+        nc.vector.memset(eps_col[:], EPS)
         hA = {}
-        shift = {}
+        hS = {}
+        sm = {}
+        nm = {}
+        sq = {}
+        stt = {}
+        mv = {}
         rstd = {}
         tt = {}
+        oo = {}
 
         def back(i):
             c = chunk_of[i]
             r = i - starts[c]
             hA[i] = []
             for a in range(2):
-                ha = psum.tile([P, 512], F32, name="hA", tag="ps", bufs=6)
+                ha = psum.tile([P, 512], F32, name="hA", tag="h%d" % (i % 2), bufs=2)
                 for jj in range(4):
                     nc.tensor.transpose(ha[:, P * jj : P * jj + P], hT[c][:, 4 * a + jj, P * r : P * r + P], ident[:])
                 hA[i].append(ha)
 
-        def stats(i):
-            ve = small.tile([P, 1], F32, name="ve")
-            rstd[i] = small.tile([P, 1], F32, name="rs")
-            if STATS[i] == "V":
-                st = small.tile([P, 2, 6], F32, name="st")
-                for a in range(2):
-                    nc.vector.bn_stats(out=st[:, a, :], in_=hA[i][a][:])
-                mv = small.tile([P, 2], F32, name="mv")
-                nc.vector.bn_aggr(out=mv[:], in_=st[:].rearrange("p a s -> p (a s)"))
-                nc.gpsimd.tensor_scalar(out=ve[:], in0=mv[:, 1:2], scalar1=1.0, scalar2=EPS, op0=ALU.mult, op1=ALU.add)
-                shift[i] = (mv[:, 0:1], ALU.subtract)
-            else:
-                sums = small.tile([P, 2], F32, name="sums")
-                for a in range(2):
-                    nc.scalar.activation(out=junk[:], in_=hA[i][a][:], func=ACT.Identity, accum_out=sums[:, a : a + 1])
-                nm = small.tile([P, 1], F32, name="nm")
-                tmp = small.tile([P, 2], F32, name="tmp")
-                nc.scalar.activation(out=tmp[:], in_=sums[:], func=ACT.Identity, scale=-1.0 / H, accum_out=nm[:])
-                ss = small.tile([P, 2], F32, name="ss")
-                for a in range(2):
-                    nc.scalar.activation(out=junk[:], in_=hA[i][a][:], func=ACT.Square, bias=nm[:], accum_out=ss[:, a : a + 1])
-                var = small.tile([P, 1], F32, name="var")
-                tmp2 = small.tile([P, 2], F32, name="tmp2")
-                nc.scalar.activation(out=tmp2[:], in_=ss[:], func=ACT.Identity, scale=1.0 / H, accum_out=var[:])
-                nm2 = small.tile([P, 1], F32, name="nm2")
-                nc.scalar.copy(out=nm2[:], in_=nm[:])
-                nc.gpsimd.tensor_scalar(out=ve[:], in0=var[:], scalar1=1.0, scalar2=EPS, op0=ALU.mult, op1=ALU.add)
-                shift[i] = (nm2[:], ALU.add)
-            nc.gpsimd.tensor_tensor(out=rstd[i][:], in0=ve[:], in1=neg_half[:], op=ALU.pow)
-
-        def centre(i):
-            tt[i] = work.tile([P, H], F32, name="t", tag="t", bufs=5)
+        def s_p1(i):
+            hS[i] = work.tile([P, H], F32, name="hS", tag="hS", bufs=3)
+            sm[i] = small.tile([P, 2], F32, name="sm")
             for a in range(2):
-                nc.vector.scalar_tensor_tensor(
-                    out=tt[i][:, 512 * a : 512 * a + 512],
-                    in0=hA[i][a][:],
-                    scalar=shift[i][0],
-                    in1=gb[:, 512 * a : 512 * a + 512],
-                    op0=shift[i][1],
-                    op1=ALU.mult,
+                nc.scalar.activation(
+                    out=hS[i][:, 512 * a : 512 * a + 512], in_=hA[i][a][:], func=ACT.Identity, accum_out=sm[i][:, a : a + 1]
                 )
 
-        def finish(i):
-            o = work.tile([P, H], F32, name="o", tag="o", bufs=4)
+        def s_nm(i):
+            nm[i] = small.tile([P, 1], F32, name="nm")
+            tmp = small.tile([P, 2], F32, name="tmp")
+            nc.scalar.activation(out=tmp[:], in_=sm[i][:], func=ACT.Identity, scale=-1.0 / H, accum_out=nm[i][:])
+
+        def s_p2(i):
+            sq[i] = small.tile([P, 1], F32, name="sq")
+            nc.scalar.activation(out=junk[:], in_=hS[i][:], func=ACT.Square, bias=nm[i][:], accum_out=sq[i][:])
+
+        def s_ve(i):
+            ve = small.tile([P, 1], F32, name="ve")
+            nc.scalar.activation(out=ve[:], in_=sq[i][:], func=ACT.Identity, scale=1.0 / H, bias=eps_col[:])
+            rstd[i] = small.tile([P, 1], F32, name="rs")
+            nc.gpsimd.tensor_tensor(out=rstd[i][:], in0=ve[:], in1=neg_half[:], op=ALU.pow)
+
+        def v_bs(i):
+            stt[i] = small.tile([P, 2, 6], F32, name="st")
+            for a in range(2):
+                nc.vector.bn_stats(out=stt[i][:, a, :], in_=hA[i][a][:])
+
+        def v_ag(i):
+            mv[i] = small.tile([P, 2], F32, name="mv")
+            nc.vector.bn_aggr(out=mv[i][:], in_=stt[i][:].rearrange("p a s -> p (a s)"))
+            ve = small.tile([P, 1], F32, name="ve")
+            nc.gpsimd.tensor_scalar(out=ve[:], in0=mv[i][:, 1:2], scalar1=1.0, scalar2=EPS, op0=ALU.mult, op1=ALU.add)
+            rstd[i] = small.tile([P, 1], F32, name="rs")
+            nc.gpsimd.tensor_tensor(out=rstd[i][:], in0=ve[:], in1=neg_half[:], op=ALU.pow)
+
+        def ce(i):
+            tt[i] = work.tile([P, H], F32, name="t", tag="t", bufs=4)
+            if STATS[i] == "V":
+                for a in range(2):
+                    nc.vector.scalar_tensor_tensor(
+                        out=tt[i][:, 512 * a : 512 * a + 512],
+                        in0=hA[i][a][:],
+                        scalar=mv[i][:, 0:1],
+                        in1=gb[:, 512 * a : 512 * a + 512],
+                        op0=ALU.subtract,
+                        op1=ALU.mult,
+                    )
+            else:
+                nc.vector.scalar_tensor_tensor(
+                    out=tt[i][:], in0=hS[i][:], scalar=nm[i][:], in1=gb[:, 0:H], op0=ALU.add, op1=ALU.mult
+                )
+
+        def fin(i, a):
+            if i < 0:
+                return
+            if a == 0:
+                oo[i] = work.tile([P, H], F32, name="o", tag="o", bufs=3)
+            cols = slice(512 * a, 512 * a + 512)
             nc.vector.scalar_tensor_tensor(
-                out=o[:], in0=tt[i][:], scalar=rstd[i][:], in1=gb[:, H : 2 * H], op0=ALU.mult, op1=ALU.add
+                out=oo[i][:, cols], in0=tt[i][:, cols], scalar=rstd[i][:], in1=gb[:, H + 512 * a : H + 512 * a + 512],
+                op0=ALU.mult, op1=ALU.add,
             )
-            nc.sync.dma_start(out=out[P * i : P * i + P, :], in_=o[:])
+            if a == 1:
+                c = chunk_of[i]
+                n = CHUNKS[c]
+                rows_c = out[P * starts[c] : P * (starts[c] + n), :].rearrange("(p r) h -> p r h", r=n)
+                nc.sync.dma_start(out=rows_c[:, i - starts[c], :], in_=oo[i][:])
+
+        groups = [(c, j) for c in range(len(CHUNKS)) for j in range(NJ)]
+        made = [0, 0]
+
+        def make(n):
+            for q in range(n):
+                if made[0] < len(groups):
+                    mx(groups[made[0]][0], groups[made[0]][1])
+                    made[0] += 1
+
+        def act(n=1):
+            for q in range(n):
+                if made[1] < len(groups):
+                    silu(groups[made[1]][0], groups[made[1]][1])
+                    made[1] += 1
 
         def x_plan(tiles):
             for i in tiles:
-                x_prep(i)
+                x_turn(i)
+                x_exit(i)
                 c = chunk_of[i]
                 if i == starts[c] + CHUNKS[c] - 1:
                     x_quant(c)
+
+        def backs(k):
+            if 2 * k < NT and not turned[k] and made[1] >= NJ * (chunk_of[2 * k] + 1):
+                back(2 * k)
+                back(2 * k + 1)
+                turned[k] = True
+
+        turned = [False] * (NT // 2)
+
+        def am():
+            act()
+            make(1)
 
         w_regroup(0, 0)
         w_regroup(0, 1)
@@ -226,36 +300,83 @@ def tile_evidentialhead_pa_kernel(tc, x, W1, b1, g, beta, out):
         w_quant(0, 1)
         w_regroup(1, 1)
         w_quant(1, 0)
-        x_prep(0)
-        x_prep(1)
+        x_turn(0)
+        x_exit(0)
+        x_turn(1)
+        x_exit(1)
         w_quant(1, 1)
         x_quant(0)
-        x_plan(XPLAN[0][2:])
-        for j in range(NJ):
-            mx_group(0, j)
-        for k in range(NT // 2):
-            pair = [2 * k, 2 * k + 1]
-            c = chunk_of[pair[0]]
-            n = CHUNKS[c] // 2
-            r = (pair[0] - starts[c]) // 2
-            for i in pair:
-                back(i)
-            for i in pair:
-                if STATS[i] == "S":
-                    stats(i)
-            if c + 1 < len(CHUNKS):
-                for j in range(NJ * r // n, NJ * (r + 1) // n):
-                    mx_group(c + 1, j)
-            for i in pair:
-                if STATS[i] == "V":
-                    stats(i)
-                    centre(i)
-            if k > 0:
-                finish(pair[0] - 2)
-                finish(pair[1] - 2)
-            for i in pair:
-                if STATS[i] == "S":
-                    centre(i)
-            x_plan(XPLAN[k + 1])
-        finish(NT - 2)
-        finish(NT - 1)
+        x_plan([2, 3])
+        for i in (4, 5, 6, 7):
+            x_turn(i)
+        make(2)
+        x_turn(8)
+        for i in (4, 5, 6, 7):
+            x_exit(i)
+        x_quant(2)
+        for n in range(8):
+            make(1)
+            act()
+            make(1)
+            act()
+            if n < 7:
+                x_turn(9 + n)
+            x_exit(8 + n)
+            if n == 3:
+                x_quant(3)
+                backs(0)
+                v_bs(0)
+                v_bs(1)
+                v_ag(0)
+            if n == 4:
+                ce(0)
+                v_ag(1)
+            if n == 5:
+                ce(1)
+        x_quant(4)
+        make(2)
+        backs(1)
+        for k in range(1, NT // 2):
+            e, o = 2 * k, 2 * k + 1
+            if STATS[o] == "V":
+                for q in range(SHARE[k] - 2):
+                    am()
+                s_p1(e)
+                v_bs(o)
+                am()
+                s_nm(e)
+                fin(e - 2, 0)
+                fin(e - 2, 1)
+                v_ag(o)
+                am()
+                s_p2(e)
+                fin(o - 2, 0)
+                ce(o)
+                backs(k + 1)
+                s_ve(e)
+                fin(o - 2, 1)
+                ce(e)
+            else:
+                for q in range(SHARE[k] - 2):
+                    am()
+                s_p1(e)
+                s_p1(o)
+                backs(k + 1)
+                s_nm(e)
+                am()
+                s_nm(o)
+                fin(e - 2, 0)
+                fin(e - 2, 1)
+                s_p2(e)
+                fin(o - 2, 0)
+                fin(o - 2, 1)
+                s_p2(o)
+                ce(e)
+                s_ve(e)
+                am()
+                s_ve(o)
+                ce(o)
+                backs(k + 1)
+        for i in (NT - 2, NT - 1):
+            fin(i, 0)
+            fin(i, 1)

@@ -21,11 +21,11 @@ NJ = H // P
 
 CHUNKS = [2, 2, 4, 4, 4]
 XEXIT = "SSSSVVVVSSSSSSSS"
-STATS = "VVSVSSSVSSSVSSSS"
+STATS = "VVSVSVSVSSSVSVSS"
 ACC = 4
 SHARE = [0, 8, 4, 4, 4, 4, 0, 0]
 WV = 336
-PIN = True
+PIN = False
 
 
 def tile_evidentialhead_pa_kernel(tc, x, W1, b1, g, beta, out):
@@ -70,19 +70,27 @@ def tile_evidentialhead_pa_kernel(tc, x, W1, b1, g, beta, out):
             xr.append(xc)
 
         gb = const.tile([P, 2 * H], F32, name="gb")
-        for n in range(4):
-            bc = psum.tile([P, 512], F32, name="bc", tag="acc", bufs=ACC)
-            nc.tensor.matmul(out=bc[:], lhsT=ones[:], rhs=rows[:, 512 * n : 512 * n + 512], start=True, stop=True)
-            if n % 2 == 0:
-                nc.vector.tensor_copy(out=gb[:, 512 * n : 512 * n + 512], in_=bc[:])
-            else:
-                nc.scalar.copy(out=gb[:, 512 * n : 512 * n + 512], in_=bc[:])
+        bcs = []
+
+        def spread_mm():
+            for n in range(4):
+                bc = psum.tile([P, 512], F32, name="bc", tag="h%d" % (n % 2), bufs=2)
+                nc.tensor.matmul(out=bc[:], lhsT=ones[:], rhs=rows[:, 512 * n : 512 * n + 512], start=True, stop=True)
+                bcs.append(bc)
+
+        def spread_out(n):
+            nc.scalar.copy(out=gb[:, 512 * n : 512 * n + 512], in_=bcs[n][:])
+
         b1f = const.tile([P, P], F32, name="b1f")
-        nc.vector.tensor_copy(out=b1f[:], in_=rows[:, 2 * H : 2 * H + P])
-        b1p = psum.tile([P, 4, P], F32, name="b1p", tag="acc", bufs=ACC)
-        nc.tensor.transpose(b1p[:, 0, :], b1f[:], ident[:])
         b1T = const.tile([P, NJ], F32, name="b1T")
-        nc.vector.tensor_copy(out=b1T[:], in_=b1p[:, 0, 0:NJ])
+        b1p = psum.tile([P, 4, P], F32, name="b1p", tag="acc", bufs=ACC)
+
+        def bias_a():
+            nc.vector.tensor_copy(out=b1f[:], in_=rows[:, 2 * H : 2 * H + P])
+            nc.tensor.transpose(b1p[:, 0, :], b1f[:], ident[:])
+
+        def bias_b():
+            nc.vector.tensor_copy(out=b1T[:], in_=b1p[:, 0, 0:NJ])
 
         wg = wpool.tile([P, 2, H, 4], BF16, name="wg", align_bytes=64)
         wq = wpool.tile([P, 2, H], U32, name="wq", align_bytes=64)
@@ -293,9 +301,11 @@ def tile_evidentialhead_pa_kernel(tc, x, W1, b1, g, beta, out):
             act()
             make(1)
 
+        bias_a()
         w_regroup(0, 0)
         w_regroup(0, 1)
         w_quant(0, 0)
+        bias_b()
         w_regroup(1, 0)
         w_quant(0, 1)
         w_regroup(1, 1)
@@ -307,6 +317,9 @@ def tile_evidentialhead_pa_kernel(tc, x, W1, b1, g, beta, out):
         w_quant(1, 1)
         x_quant(0)
         x_plan([2, 3])
+        spread_mm()
+        for n in range(4):
+            spread_out(n)
         for i in (4, 5, 6, 7):
             x_turn(i)
         make(2)
@@ -323,7 +336,6 @@ def tile_evidentialhead_pa_kernel(tc, x, W1, b1, g, beta, out):
                 x_turn(9 + n)
             x_exit(8 + n)
             if n == 3:
-                x_quant(3)
                 backs(0)
                 v_bs(0)
                 v_bs(1)
@@ -333,6 +345,7 @@ def tile_evidentialhead_pa_kernel(tc, x, W1, b1, g, beta, out):
                 v_ag(1)
             if n == 5:
                 ce(1)
+                x_quant(3)
         x_quant(4)
         make(2)
         backs(1)

@@ -21,7 +21,7 @@ NJ = H // P
 
 CHUNKS = [2, 2, 4, 4, 4]
 XEXIT = "SSSSVVVVSSSSSSSS"
-STATS = "VVSVSVSVSSSVSVSS"
+STATS = "VVSVSVSVSVSVSSSS"
 ACC = 4
 SHARE = [0, 8, 4, 4, 4, 4, 0, 0]
 WV = 336
@@ -74,7 +74,7 @@ def tile_evidentialhead_pa_kernel(tc, x, W1, b1, g, beta, out):
 
         def spread_mm():
             for n in range(4):
-                bc = psum.tile([P, 512], F32, name="bc", tag="h%d" % (n % 2), bufs=2)
+                bc = psum.tile([P, 512], F32, name="bc", tag="ps", bufs=8)
                 nc.tensor.matmul(out=bc[:], lhsT=ones[:], rhs=rows[:, 512 * n : 512 * n + 512], start=True, stop=True)
                 bcs.append(bc)
 
@@ -83,7 +83,7 @@ def tile_evidentialhead_pa_kernel(tc, x, W1, b1, g, beta, out):
 
         b1f = const.tile([P, P], F32, name="b1f")
         b1T = const.tile([P, NJ], F32, name="b1T")
-        b1p = psum.tile([P, 4, P], F32, name="b1p", tag="acc", bufs=ACC)
+        b1p = psum.tile([P, 4, P], F32, name="b1p", tag="ps", bufs=8)
 
         def bias_a():
             nc.vector.tensor_copy(out=b1f[:], in_=rows[:, 2 * H : 2 * H + P])
@@ -125,7 +125,7 @@ def tile_evidentialhead_pa_kernel(tc, x, W1, b1, g, beta, out):
             nb = P * CHUNKS[c]
             if r == 0:
                 xg[c] = work.tile([P, 8 * nb], BF16, name="xg", tag="xg", bufs=2, align_bytes=64)
-            xt = psum.tile([P, 4, P], F32, name="xt", tag=("h%d" % (i % 2) if XEXIT[i] == "V" else "acc"), bufs=(2 if XEXIT[i] == "V" else ACC))
+            xt = psum.tile([P, 4, P], F32, name="xt", tag="ps", bufs=8)
             xw = xr[c][:, r, :].bitcast(F32)
             for w in range(4):
                 nc.tensor.transpose(xt[:, w, :], xw[:, P * w : P * w + P], ident[:])
@@ -154,7 +154,7 @@ def tile_evidentialhead_pa_kernel(tc, x, W1, b1, g, beta, out):
             nb = P * CHUNKS[c]
             if j == 0:
                 hT[c] = work.tile([P, NJ, nb], F32, name="hT", tag="hT", bufs=3)
-            acc = psum.tile([P, 512], F32, name="acc", tag="acc", bufs=ACC)
+            acc = psum.tile([P, 512], F32, name="acc", tag="ps", bufs=8)
             for gi in range(2):
                 nc.tensor.matmul_mx(
                     out=acc[:, 0:nb],
@@ -192,7 +192,7 @@ def tile_evidentialhead_pa_kernel(tc, x, W1, b1, g, beta, out):
             r = i - starts[c]
             hA[i] = []
             for a in range(2):
-                ha = psum.tile([P, 512], F32, name="hA", tag="h%d" % (i % 2), bufs=2)
+                ha = psum.tile([P, 512], F32, name="hA", tag="ps", bufs=8)
                 for jj in range(4):
                     nc.tensor.transpose(ha[:, P * jj : P * jj + P], hT[c][:, 4 * a + jj, P * r : P * r + P], ident[:])
                 hA[i].append(ha)

@@ -18,29 +18,25 @@ EPS = 1e-5
 FLOPS = 2 * B * D * H
 NT = B // P
 NJ = H // P
-
-CHUNKS = [2, 2, 4, 4, 4]
-XEXIT = "SSSSVVVVSSSSSSSS"
-STATS = "VVSVSVSVSVSVSSSS"
-ACC = 4
-SHARE = [0, 8, 4, 4, 4, 4, 0, 0]
-WV = 336
-PIN = False
+BANK = 512
+CHUNKS = (2, 2, 2, 2, 2, 2, 2, 2)
+VLIM = 12
+XV = (2,)
+W_VECTOR_COLS = 336
 
 
 def tile_evidentialhead_pa_kernel(tc, x, W1, b1, g, beta, out):
     nc = tc.nc
     starts = [sum(CHUNKS[:c]) for c in range(len(CHUNKS))]
-    chunk_of = [max(k for k in range(len(CHUNKS)) if starts[k] <= i) for i in range(NT)]
+    chunk_of = [c for c, n in enumerate(CHUNKS) for r in range(n)]
     with ExitStack() as ctx:
         const = ctx.enter_context(tc.tile_pool(name="const", bufs=1))
-        wpool = ctx.enter_context(tc.tile_pool(name="wpool", bufs=1))
-        xpool = ctx.enter_context(tc.tile_pool(name="xpool", bufs=1))
         work = ctx.enter_context(tc.tile_pool(name="work", bufs=2))
         small = ctx.enter_context(tc.tile_pool(name="small", bufs=6))
-        psum = ctx.enter_context(tc.psum_pool(name="psum", bufs=2))
-        if PIN:
-            ctx.enter_context(tc.manual_schedule())
+        psum = ctx.enter_context(tc.psum_pool(name="psum", bufs=8))
+
+        def bank(name):
+            return psum.tile([P, BANK], F32, name=name, tag="bank")
 
         rows = const.tile([P, 2 * H + P], BF16, name="rows")
         nc.vector.memset(rows[:].bitcast(I32), 0)
@@ -48,348 +44,184 @@ def tile_evidentialhead_pa_kernel(tc, x, W1, b1, g, beta, out):
         nc.vector.memset(ones[:], 1.0)
         neg_half = const.tile([P, 1], F32, name="neg_half")
         nc.vector.memset(neg_half[:], -0.5)
+        eps_col = const.tile([P, 1], F32, name="eps_col")
+        nc.vector.memset(eps_col[:], EPS)
         ident = const.tile([P, P], F32, name="ident")
         make_identity(nc, ident[:])
+        warm = const.tile([P, 1], F32, name="warm")
+        nc.scalar.activation(out=warm[:], in_=neg_half[:], func=ACT.Silu)
         nc.scalar.dma_start(out=rows[0:1, 0:H], in_=g.unsqueeze(0))
         nc.scalar.dma_start(out=rows[0:1, H : 2 * H], in_=beta.unsqueeze(0))
         nc.scalar.dma_start(out=rows[0:NJ, 2 * H : 2 * H + P], in_=b1.rearrange("(j m) -> j m", m=P))
 
-        wraw = wpool.tile([P, 8, H], BF16, name="wraw")
+        w_raw = const.tile([P, 8, H], BF16, name="w_raw")
         for w in range(4):
             nc.sync.dma_start(
-                out=wraw[:, 2 * w : 2 * w + 2, :],
+                out=w_raw[:, 2 * w : 2 * w + 2, :],
                 in_=W1[256 * w : 256 * w + 256, :].rearrange("(p e) c -> p e c", e=2),
             )
-        xr = []
-        for c in range(len(CHUNKS)):
-            n = CHUNKS[c]
-            xc = xpool.tile([P, n, D], BF16, name="x%d" % c)
+        x_raw = []
+        for c, n in enumerate(CHUNKS):
+            xc = const.tile([P, n, D], BF16, name="x_raw%d" % c)
             nc.sync.dma_start(
                 out=xc[:], in_=x[P * starts[c] : P * (starts[c] + n), :].rearrange("(p r) k -> p r k", r=n)
             )
-            xr.append(xc)
+            x_raw.append(xc)
 
-        gb = const.tile([P, 2 * H], F32, name="gb")
-        bcs = []
+        b1_rows = const.tile([P, P], F32, name="b1_rows")
+        nc.vector.tensor_copy(out=b1_rows[:], in_=rows[:, 2 * H : 2 * H + P])
+        b1_bank = bank("b1_bank")
+        nc.tensor.transpose(b1_bank[:, 0:P], b1_rows[:], ident[:])
+        b1_col = const.tile([P, NJ], F32, name="b1_col")
+        nc.vector.tensor_copy(out=b1_col[:], in_=b1_bank[:, 0:NJ])
 
-        def spread_mm():
-            for n in range(4):
-                bc = psum.tile([P, 512], F32, name="bc", tag="ps", bufs=8)
-                nc.tensor.matmul(out=bc[:], lhsT=ones[:], rhs=rows[:, 512 * n : 512 * n + 512], start=True, stop=True)
-                bcs.append(bc)
+        w_grouped = const.tile([P, 2, H, 4], BF16, name="w_grouped", align_bytes=64)
+        w_codes = const.tile([P, 2, H], U32, name="w_codes", align_bytes=64)
+        w_scales = const.tile([P, 2, H], U8, name="w_scales", align_bytes=64)
+        for gi in range(2):
+            for lo in (0, BANK):
+                cut = lo + W_VECTOR_COLS
+                for copy, a, b in ((nc.vector.tensor_copy, lo, cut), (nc.scalar.copy, cut, lo + BANK)):
+                    copy(
+                        out=w_grouped[:, gi, a:b, :].rearrange("p (c i) t -> p c t i", i=4),
+                        in_=w_raw[:, 4 * gi : 4 * gi + 4, a:b].rearrange("p t (c i) -> p c t i", i=4),
+                    )
+            for lo in (0, BANK):
+                nc.vector.quantize_mx(
+                    out=w_codes[:, gi, lo : lo + BANK].bitcast(FP8X4),
+                    scales=w_scales[:, gi, lo : lo + BANK],
+                    in_=w_grouped[:, gi, lo : lo + BANK, :].rearrange("p c t -> p (c t)"),
+                )
 
-        def spread_out(n):
-            nc.scalar.copy(out=gb[:, 512 * n : 512 * n + 512], in_=bcs[n][:])
+        x_codes = {}
+        x_scales = {}
 
-        b1f = const.tile([P, P], F32, name="b1f")
-        b1T = const.tile([P, NJ], F32, name="b1T")
-        b1p = psum.tile([P, 4, P], F32, name="b1p", tag="ps", bufs=8)
-
-        def bias_a():
-            nc.vector.tensor_copy(out=b1f[:], in_=rows[:, 2 * H : 2 * H + P])
-            nc.tensor.transpose(b1p[:, 0, :], b1f[:], ident[:])
-
-        def bias_b():
-            nc.vector.tensor_copy(out=b1T[:], in_=b1p[:, 0, 0:NJ])
-
-        wg = wpool.tile([P, 2, H, 4], BF16, name="wg", align_bytes=64)
-        wq = wpool.tile([P, 2, H], U32, name="wq", align_bytes=64)
-        ws = wpool.tile([P, 2, H], U8, name="ws", align_bytes=64)
-
-        def w_regroup(gi, h):
-            for eng, lo, hi in (("V", 512 * h, 512 * h + WV), ("S", 512 * h + WV, 512 * h + 512)):
-                dst = wg[:, gi, lo:hi, :].rearrange("p (c i) t -> p c t i", i=4)
-                src = wraw[:, 4 * gi : 4 * gi + 4, lo:hi].rearrange("p t (c i) -> p c t i", i=4)
-                if eng == "V":
-                    nc.vector.tensor_copy(out=dst, in_=src)
-                else:
-                    nc.scalar.copy(out=dst, in_=src)
-
-        def w_quant(gi, h):
-            cols = slice(512 * h, 512 * h + 512)
-            nc.vector.quantize_mx(
-                out=wq[:, gi, cols].bitcast(FP8X4),
-                scales=ws[:, gi, cols],
-                in_=wg[:, gi, cols, :].rearrange("p c t -> p (c t)"),
-            )
-
-        xg = {}
-        xq = {}
-        xs = {}
-
-        xts = {}
-
-        def x_turn(i):
-            c = chunk_of[i]
-            r = i - starts[c]
-            nb = P * CHUNKS[c]
-            if r == 0:
-                xg[c] = work.tile([P, 8 * nb], BF16, name="xg", tag="xg", bufs=2, align_bytes=64)
-            xt = psum.tile([P, 4, P], F32, name="xt", tag="ps", bufs=8)
-            xw = xr[c][:, r, :].bitcast(F32)
-            for w in range(4):
-                nc.tensor.transpose(xt[:, w, :], xw[:, P * w : P * w + P], ident[:])
-            xts[i] = xt
-
-        def x_exit(i):
-            c = chunk_of[i]
-            r = i - starts[c]
-            dst = xg[c][:].bitcast(F32).rearrange("p (g b u) -> p g b u", g=2, u=2)[:, :, P * r : P * r + P, :]
-            src = xts[i][:].rearrange("p (g u) b -> p g b u", g=2)
-            if XEXIT[i] == "V":
-                nc.vector.tensor_copy(out=dst, in_=src)
-            else:
-                nc.scalar.copy(out=dst, in_=src)
-
-        def x_quant(c):
-            nb = P * CHUNKS[c]
-            xq[c] = xpool.tile([P, 2 * nb], U32, name="xq%d" % c, align_bytes=64)
-            xs[c] = xpool.tile([P, 2 * nb], U8, name="xs%d" % c, align_bytes=64)
-            nc.vector.quantize_mx(out=xq[c][:].bitcast(FP8X4), scales=xs[c][:], in_=xg[c][:])
+        def prepare_x(c, copy):
+            n = CHUNKS[c]
+            nb = P * n
+            grouped = work.tile([P, 8 * nb], BF16, name="x_grouped", tag="x_grouped", bufs=3, align_bytes=64)
+            for r in range(n):
+                turned = bank("x_turned")
+                words = x_raw[c][:, r, :].bitcast(F32)
+                for w in range(4):
+                    nc.tensor.transpose(turned[:, P * w : P * w + P], words[:, P * w : P * w + P], ident[:])
+                copy(
+                    out=grouped[:].bitcast(F32).rearrange("p (g b u) -> p g b u", g=2, u=2)[:, :, P * r : P * r + P, :],
+                    in_=turned[:].rearrange("p (g u b) -> p g b u", g=2, u=2),
+                )
+            x_codes[c] = const.tile([P, 2 * nb], U32, name="x_codes%d" % c, align_bytes=64)
+            x_scales[c] = const.tile([P, 2 * nb], U8, name="x_scales%d" % c, align_bytes=64)
+            nc.vector.quantize_mx(out=x_codes[c][:].bitcast(FP8X4), scales=x_scales[c][:], in_=grouped[:])
 
         hT = {}
-        accs = {}
 
-        def mx(c, j):
+        def produce(c, js):
             nb = P * CHUNKS[c]
-            if j == 0:
-                hT[c] = work.tile([P, NJ, nb], F32, name="hT", tag="hT", bufs=3)
-            acc = psum.tile([P, 512], F32, name="acc", tag="ps", bufs=8)
-            for gi in range(2):
-                nc.tensor.matmul_mx(
-                    out=acc[:, 0:nb],
-                    lhsT=wq[:, gi, P * j : P * j + P].bitcast(FP8X4),
-                    lhsT_scale=ws[:, gi, P * j : P * j + P],
-                    rhs=xq[c][:, nb * gi : nb * gi + nb].bitcast(FP8X4),
-                    rhs_scale=xs[c][:, nb * gi : nb * gi + nb],
-                    start=(gi == 0),
-                    stop=(gi == 1),
+            for j in js:
+                if j == 0:
+                    hT[c] = work.tile([P, NJ, nb], F32, name="hT", tag="hT", bufs=4)
+                acc = bank("acc")
+                for gi in range(2):
+                    nc.tensor.matmul_mx(
+                        out=acc[:, 0:nb],
+                        lhsT=w_codes[:, gi, P * j : P * j + P].bitcast(FP8X4),
+                        lhsT_scale=w_scales[:, gi, P * j : P * j + P],
+                        rhs=x_codes[c][:, nb * gi : nb * gi + nb].bitcast(FP8X4),
+                        rhs_scale=x_scales[c][:, nb * gi : nb * gi + nb],
+                        start=(gi == 0),
+                        stop=(gi == 1),
+                    )
+                nc.scalar.activation(
+                    out=hT[c][:, j, :], in_=acc[:, 0:nb], func=ACT.Silu, bias=b1_col[:, j : j + 1], scale=1.0
                 )
-            accs[(c, j)] = acc
 
-        def silu(c, j):
-            nb = P * CHUNKS[c]
-            nc.scalar.activation(
-                out=hT[c][:, j, :], in_=accs[(c, j)][:, 0:nb], func=ACT.Silu, bias=b1T[:, j : j + 1], scale=1.0
-            )
+        gb = const.tile([P, 2 * H], F32, name="gb")
+
+        def spread_g_beta():
+            for q in range(4):
+                spread = bank("spread")
+                nc.tensor.matmul(
+                    out=spread[:], lhsT=ones[:], rhs=rows[:, BANK * q : BANK * q + BANK], start=True, stop=True
+                )
+                nc.scalar.copy(out=gb[:, BANK * q : BANK * q + BANK], in_=spread[:])
 
         junk = const.tile([P, H], F32, name="junk")
-        eps_col = const.tile([P, 1], F32, name="eps_col")
-        nc.vector.memset(eps_col[:], EPS)
-        hA = {}
-        hS = {}
-        sm = {}
-        nm = {}
-        sq = {}
-        stt = {}
-        mv = {}
+        centred = {}
         rstd = {}
-        tt = {}
-        oo = {}
 
-        def back(i):
+        def centre(i):
             c = chunk_of[i]
             r = i - starts[c]
-            hA[i] = []
+            halves = []
             for a in range(2):
-                ha = psum.tile([P, 512], F32, name="hA", tag="ps", bufs=8)
+                half = bank("h_half")
                 for jj in range(4):
-                    nc.tensor.transpose(ha[:, P * jj : P * jj + P], hT[c][:, 4 * a + jj, P * r : P * r + P], ident[:])
-                hA[i].append(ha)
-
-        def s_p1(i):
-            hS[i] = work.tile([P, H], F32, name="hS", tag="hS", bufs=3)
-            sm[i] = small.tile([P, 2], F32, name="sm")
-            for a in range(2):
-                nc.scalar.activation(
-                    out=hS[i][:, 512 * a : 512 * a + 512], in_=hA[i][a][:], func=ACT.Identity, accum_out=sm[i][:, a : a + 1]
-                )
-
-        def s_nm(i):
-            nm[i] = small.tile([P, 1], F32, name="nm")
-            tmp = small.tile([P, 2], F32, name="tmp")
-            nc.scalar.activation(out=tmp[:], in_=sm[i][:], func=ACT.Identity, scale=-1.0 / H, accum_out=nm[i][:])
-
-        def s_p2(i):
-            sq[i] = small.tile([P, 1], F32, name="sq")
-            nc.scalar.activation(out=junk[:], in_=hS[i][:], func=ACT.Square, bias=nm[i][:], accum_out=sq[i][:])
-
-        def s_ve(i):
-            ve = small.tile([P, 1], F32, name="ve")
-            nc.scalar.activation(out=ve[:], in_=sq[i][:], func=ACT.Identity, scale=1.0 / H, bias=eps_col[:])
-            rstd[i] = small.tile([P, 1], F32, name="rs")
-            nc.gpsimd.tensor_tensor(out=rstd[i][:], in0=ve[:], in1=neg_half[:], op=ALU.pow)
-
-        def v_bs(i):
-            stt[i] = small.tile([P, 2, 6], F32, name="st")
-            for a in range(2):
-                nc.vector.bn_stats(out=stt[i][:, a, :], in_=hA[i][a][:])
-
-        def v_ag(i):
-            mv[i] = small.tile([P, 2], F32, name="mv")
-            nc.vector.bn_aggr(out=mv[i][:], in_=stt[i][:].rearrange("p a s -> p (a s)"))
-            ve = small.tile([P, 1], F32, name="ve")
-            nc.gpsimd.tensor_scalar(out=ve[:], in0=mv[i][:, 1:2], scalar1=1.0, scalar2=EPS, op0=ALU.mult, op1=ALU.add)
-            rstd[i] = small.tile([P, 1], F32, name="rs")
-            nc.gpsimd.tensor_tensor(out=rstd[i][:], in0=ve[:], in1=neg_half[:], op=ALU.pow)
-
-        def ce(i):
-            tt[i] = work.tile([P, H], F32, name="t", tag="t", bufs=4)
-            if STATS[i] == "V":
+                    nc.tensor.transpose(half[:, P * jj : P * jj + P], hT[c][:, 4 * a + jj, P * r : P * r + P], ident[:])
+                halves.append(half)
+            t = work.tile([P, H], F32, name="centred", tag="centred", bufs=5)
+            var_eps = small.tile([P, 1], F32, name="var_eps")
+            if (i == 0 or i % 2 == 1) and i < VLIM:
+                stats = small.tile([P, 2, 6], F32, name="stats")
                 for a in range(2):
+                    nc.vector.bn_stats(out=stats[:, a, :], in_=halves[a][:])
+                mean_var = small.tile([P, 2], F32, name="mean_var")
+                nc.vector.bn_aggr(out=mean_var[:], in_=stats[:].rearrange("p a s -> p (a s)"))
+                nc.gpsimd.tensor_scalar(
+                    out=var_eps[:], in0=mean_var[:, 1:2], scalar1=1.0, scalar2=EPS, op0=ALU.mult, op1=ALU.add
+                )
+                for a in range(2):
+                    cols = slice(BANK * a, BANK * a + BANK)
                     nc.vector.scalar_tensor_tensor(
-                        out=tt[i][:, 512 * a : 512 * a + 512],
-                        in0=hA[i][a][:],
-                        scalar=mv[i][:, 0:1],
-                        in1=gb[:, 512 * a : 512 * a + 512],
-                        op0=ALU.subtract,
-                        op1=ALU.mult,
+                        out=t[:, cols], in0=halves[a][:], scalar=mean_var[:, 0:1], in1=gb[:, cols],
+                        op0=ALU.subtract, op1=ALU.mult,
                     )
             else:
+                h = work.tile([P, H], F32, name="h", tag="h", bufs=4)
+                sums = small.tile([P, 2], F32, name="sums")
+                for a in range(2):
+                    nc.scalar.activation(
+                        out=h[:, BANK * a : BANK * a + BANK], in_=halves[a][:], func=ACT.Identity,
+                        accum_out=sums[:, a : a + 1],
+                    )
+                neg_mean = small.tile([P, 1], F32, name="neg_mean")
+                parts = small.tile([P, 2], F32, name="parts")
+                nc.scalar.activation(out=parts[:], in_=sums[:], func=ACT.Identity, scale=-1.0 / H, accum_out=neg_mean[:])
+                sum_sq = small.tile([P, 1], F32, name="sum_sq")
+                nc.scalar.activation(out=junk[:], in_=h[:], func=ACT.Square, bias=neg_mean[:], accum_out=sum_sq[:])
+                nc.scalar.activation(out=var_eps[:], in_=sum_sq[:], func=ACT.Identity, scale=1.0 / H, bias=eps_col[:])
                 nc.vector.scalar_tensor_tensor(
-                    out=tt[i][:], in0=hS[i][:], scalar=nm[i][:], in1=gb[:, 0:H], op0=ALU.add, op1=ALU.mult
+                    out=t[:], in0=h[:], scalar=neg_mean[:], in1=gb[:, 0:H], op0=ALU.add, op1=ALU.mult
                 )
+            rstd[i] = small.tile([P, 1], F32, name="rstd")
+            nc.gpsimd.tensor_tensor(out=rstd[i][:], in0=var_eps[:], in1=neg_half[:], op=ALU.pow)
+            centred[i] = t
 
-        def fin(i, a):
-            if i < 0:
-                return
-            if a == 0:
-                oo[i] = work.tile([P, H], F32, name="o", tag="o", bufs=3)
-            cols = slice(512 * a, 512 * a + 512)
+        def finish(i):
+            c = chunk_of[i]
+            n = CHUNKS[c]
+            o = work.tile([P, H], F32, name="o", tag="o", bufs=4)
             nc.vector.scalar_tensor_tensor(
-                out=oo[i][:, cols], in0=tt[i][:, cols], scalar=rstd[i][:], in1=gb[:, H + 512 * a : H + 512 * a + 512],
-                op0=ALU.mult, op1=ALU.add,
+                out=o[:], in0=centred[i][:], scalar=rstd[i][:], in1=gb[:, H : 2 * H], op0=ALU.mult, op1=ALU.add
             )
-            if a == 1:
-                c = chunk_of[i]
-                n = CHUNKS[c]
-                rows_c = out[P * starts[c] : P * (starts[c] + n), :].rearrange("(p r) h -> p r h", r=n)
-                nc.sync.dma_start(out=rows_c[:, i - starts[c], :], in_=oo[i][:])
+            rows_c = out[P * starts[c] : P * (starts[c] + n), :].rearrange("(p r) h -> p r h", r=n)
+            nc.sync.dma_start(out=rows_c[:, i - starts[c], :], in_=o[:])
 
-        groups = [(c, j) for c in range(len(CHUNKS)) for j in range(NJ)]
-        made = [0, 0]
-
-        def make(n):
-            for q in range(n):
-                if made[0] < len(groups):
-                    mx(groups[made[0]][0], groups[made[0]][1])
-                    made[0] += 1
-
-        def act(n=1):
-            for q in range(n):
-                if made[1] < len(groups):
-                    silu(groups[made[1]][0], groups[made[1]][1])
-                    made[1] += 1
-
-        def x_plan(tiles):
-            for i in tiles:
-                x_turn(i)
-                x_exit(i)
-                c = chunk_of[i]
-                if i == starts[c] + CHUNKS[c] - 1:
-                    x_quant(c)
-
-        def backs(k):
-            if 2 * k < NT and not turned[k] and made[1] >= NJ * (chunk_of[2 * k] + 1):
-                back(2 * k)
-                back(2 * k + 1)
-                turned[k] = True
-
-        turned = [False] * (NT // 2)
-
-        def am():
-            act()
-            make(1)
-
-        bias_a()
-        w_regroup(0, 0)
-        w_regroup(0, 1)
-        w_quant(0, 0)
-        bias_b()
-        w_regroup(1, 0)
-        w_quant(0, 1)
-        w_regroup(1, 1)
-        w_quant(1, 0)
-        x_turn(0)
-        x_exit(0)
-        x_turn(1)
-        x_exit(1)
-        w_quant(1, 1)
-        x_quant(0)
-        x_plan([2, 3])
-        spread_mm()
-        for n in range(4):
-            spread_out(n)
-        for i in (4, 5, 6, 7):
-            x_turn(i)
-        make(2)
-        x_turn(8)
-        for i in (4, 5, 6, 7):
-            x_exit(i)
-        x_quant(2)
-        for n in range(8):
-            make(1)
-            act()
-            make(1)
-            act()
-            if n < 7:
-                x_turn(9 + n)
-            x_exit(8 + n)
-            if n == 3:
-                backs(0)
-                v_bs(0)
-                v_bs(1)
-                v_ag(0)
-            if n == 4:
-                ce(0)
-                v_ag(1)
-            if n == 5:
-                ce(1)
-                x_quant(3)
-        x_quant(4)
-        make(2)
-        backs(1)
-        for k in range(1, NT // 2):
-            e, o = 2 * k, 2 * k + 1
-            if STATS[o] == "V":
-                for q in range(SHARE[k] - 2):
-                    am()
-                s_p1(e)
-                v_bs(o)
-                am()
-                s_nm(e)
-                fin(e - 2, 0)
-                fin(e - 2, 1)
-                v_ag(o)
-                am()
-                s_p2(e)
-                fin(o - 2, 0)
-                ce(o)
-                backs(k + 1)
-                s_ve(e)
-                fin(o - 2, 1)
-                ce(e)
-            else:
-                for q in range(SHARE[k] - 2):
-                    am()
-                s_p1(e)
-                s_p1(o)
-                backs(k + 1)
-                s_nm(e)
-                am()
-                s_nm(o)
-                fin(e - 2, 0)
-                fin(e - 2, 1)
-                s_p2(e)
-                fin(o - 2, 0)
-                fin(o - 2, 1)
-                s_p2(o)
-                ce(e)
-                s_ve(e)
-                am()
-                s_ve(o)
-                ce(o)
-                backs(k + 1)
-        for i in (NT - 2, NT - 1):
-            fin(i, 0)
-            fin(i, 1)
+        prepare_x(0, nc.scalar.copy)
+        prepare_x(1, nc.scalar.copy)
+        spread_g_beta()
+        prepare_x(2, nc.vector.tensor_copy)
+        produce(0, range(NJ))
+        produce(1, range(NJ))
+        for i in range(NT):
+            c = chunk_of[i]
+            n = CHUNKS[c]
+            r = i - starts[c]
+            if r == 0 and c + 3 < len(CHUNKS):
+                prepare_x(c + 3, nc.vector.tensor_copy if c + 3 in XV else nc.scalar.copy)
+            if c + 2 < len(CHUNKS):
+                produce(c + 2, range(NJ * r // n, NJ * (r + 1) // n))
+            centre(i)
+            if i >= 2:
+                finish(i - 2)
+        finish(NT - 2)
+        finish(NT - 1)

@@ -143,7 +143,7 @@ def tile_evidentialhead_pa_kernel(tc, x, W1, b1, g, beta, out):
                 nc.tensor.matmul(
                     out=spread[:], lhsT=ones[:], rhs=rows[:, BANK * q : BANK * q + BANK], start=True, stop=True
                 )
-                nc.scalar.copy(out=gb[:, BANK * q : BANK * q + BANK], in_=spread[:])
+                nc.vector.tensor_copy(out=gb[:, BANK * q : BANK * q + BANK], in_=spread[:])
 
         junk = const.tile([P, H], F32, name="junk")
         centred = {}
@@ -208,9 +208,9 @@ def tile_evidentialhead_pa_kernel(tc, x, W1, b1, g, beta, out):
 
         prepare_x(0, nc.scalar.copy)
         prepare_x(1, nc.scalar.copy)
-        spread_g_beta()
         prepare_x(2, nc.vector.tensor_copy)
         produce(0, range(NJ))
+        spread_g_beta()
         produce(1, range(NJ))
         for i in range(NT):
             c = chunk_of[i]

@@ -117,23 +117,26 @@ def tile_evidentialhead_pa_kernel(tc, x, W1, b1, g, beta, out):
 
         def produce(c, js):
             nb = P * CHUNKS[c]
-            for j in js:
-                if j == 0:
+            for j0 in js[::2]:
+                if j0 == 0:
                     hT[c] = work.tile([P, NJ, nb], F32, name="hT", tag="hT", bufs=4)
                 acc = bank("acc")
-                for gi in range(2):
-                    nc.tensor.matmul_mx(
-                        out=acc[:, 0:nb],
-                        lhsT=w_codes[:, gi, P * j : P * j + P].bitcast(FP8X4),
-                        lhsT_scale=w_scales[:, gi, P * j : P * j + P],
-                        rhs=x_codes[c][:, nb * gi : nb * gi + nb].bitcast(FP8X4),
-                        rhs_scale=x_scales[c][:, nb * gi : nb * gi + nb],
-                        start=(gi == 0),
-                        stop=(gi == 1),
+                for j in (j0, j0 + 1):
+                    for gi in range(2):
+                        nc.tensor.matmul_mx(
+                            out=acc[:, nb * (j - j0) : nb * (j - j0) + nb],
+                            lhsT=w_codes[:, gi, P * j : P * j + P].bitcast(FP8X4),
+                            lhsT_scale=w_scales[:, gi, P * j : P * j + P],
+                            rhs=x_codes[c][:, nb * gi : nb * gi + nb].bitcast(FP8X4),
+                            rhs_scale=x_scales[c][:, nb * gi : nb * gi + nb],
+                            start=(gi == 0),
+                            stop=(gi == 1),
+                        )
+                for j in (j0, j0 + 1):
+                    nc.scalar.activation(
+                        out=hT[c][:, j, :], in_=acc[:, nb * (j - j0) : nb * (j - j0) + nb], func=ACT.Silu,
+                        bias=b1_col[:, j : j + 1], scale=1.0,
                     )
-                nc.scalar.activation(
-                    out=hT[c][:, j, :], in_=acc[:, 0:nb], func=ACT.Silu, bias=b1_col[:, j : j + 1], scale=1.0
-                )
 
         gb = const.tile([P, 2 * H], F32, name="gb")
 

@@ -117,26 +117,23 @@ def tile_evidentialhead_pa_kernel(tc, x, W1, b1, g, beta, out):
 
         def produce(c, js):
             nb = P * CHUNKS[c]
-            for j0 in js[::2]:
-                if j0 == 0:
+            for j in js:
+                if j == 0:
                     hT[c] = work.tile([P, NJ, nb], F32, name="hT", tag="hT", bufs=4)
                 acc = bank("acc")
-                for j in (j0, j0 + 1):
-                    for gi in range(2):
-                        nc.tensor.matmul_mx(
-                            out=acc[:, nb * (j - j0) : nb * (j - j0) + nb],
-                            lhsT=w_codes[:, gi, P * j : P * j + P].bitcast(FP8X4),
-                            lhsT_scale=w_scales[:, gi, P * j : P * j + P],
-                            rhs=x_codes[c][:, nb * gi : nb * gi + nb].bitcast(FP8X4),
-                            rhs_scale=x_scales[c][:, nb * gi : nb * gi + nb],
-                            start=(gi == 0),
-                            stop=(gi == 1),
-                        )
-                for j in (j0, j0 + 1):
-                    nc.scalar.activation(
-                        out=hT[c][:, j, :], in_=acc[:, nb * (j - j0) : nb * (j - j0) + nb], func=ACT.Silu,
-                        bias=b1_col[:, j : j + 1], scale=1.0,
+                for gi in range(2):
+                    nc.tensor.matmul_mx(
+                        out=acc[:, 0:nb],
+                        lhsT=w_codes[:, gi, P * j : P * j + P].bitcast(FP8X4),
+                        lhsT_scale=w_scales[:, gi, P * j : P * j + P],
+                        rhs=x_codes[c][:, nb * gi : nb * gi + nb].bitcast(FP8X4),
+                        rhs_scale=x_scales[c][:, nb * gi : nb * gi + nb],
+                        start=(gi == 0),
+                        stop=(gi == 1),
                     )
+                nc.scalar.activation(
+                    out=hT[c][:, j, :], in_=acc[:, 0:nb], func=ACT.Silu, bias=b1_col[:, j : j + 1], scale=1.0
+                )
 
         gb = const.tile([P, 2 * H], F32, name="gb")
 
@@ -203,9 +200,15 @@ def tile_evidentialhead_pa_kernel(tc, x, W1, b1, g, beta, out):
             c = chunk_of[i]
             n = CHUNKS[c]
             o = work.tile([P, H], F32, name="o", tag="o", bufs=4)
-            nc.vector.scalar_tensor_tensor(
-                out=o[:], in0=centred[i][:], scalar=rstd[i][:], in1=gb[:, H : 2 * H], op0=ALU.mult, op1=ALU.add
-            )
+            if i % 2 == 0 and 2 <= i < 12:
+                nc.gpsimd.tensor_scalar(
+                    out=o[:], in0=centred[i][:], scalar1=rstd[i][:], scalar2=0.0, op0=ALU.mult, op1=ALU.add
+                )
+                nc.gpsimd.tensor_tensor(out=o[:], in0=o[:], in1=gb[:, H : 2 * H], op=ALU.add)
+            else:
+                nc.vector.scalar_tensor_tensor(
+                    out=o[:], in0=centred[i][:], scalar=rstd[i][:], in1=gb[:, H : 2 * H], op0=ALU.mult, op1=ALU.add
+                )
             rows_c = out[P * starts[c] : P * (starts[c] + n), :].rearrange("(p r) h -> p r h", r=n)
             nc.sync.dma_start(out=rows_c[:, i - starts[c], :], in_=o[:])
 

from contextlib import ExitStack

import concourse.mybir as mybir
from concourse.masks import make_identity

F32 = mybir.dt.float32
BF16 = mybir.dt.bfloat16
U32 = mybir.dt.uint32
U8 = mybir.dt.uint8
I32 = mybir.dt.int32
FP8X4 = mybir.dt.float8_e4m3fn_x4
ACT = mybir.ActivationFunctionType
ALU = mybir.AluOpType

P = 128
B, D, H = 2048, 1024, 1024
EPS = 1e-5
FLOPS = 2 * B * D * H
NT = B // P
NJ = H // P
BANK = 512
CHUNKS = (2, 2, 2, 2, 2, 2, 2, 2)
VLIM = 12
XV = (2,)
W_VECTOR_COLS = 336


def tile_evidentialhead_pa_kernel(tc, x, W1, b1, g, beta, out):
    nc = tc.nc
    starts = [sum(CHUNKS[:c]) for c in range(len(CHUNKS))]
    chunk_of = [c for c, n in enumerate(CHUNKS) for r in range(n)]
    with ExitStack() as ctx:
        const = ctx.enter_context(tc.tile_pool(name="const", bufs=1))
        work = ctx.enter_context(tc.tile_pool(name="work", bufs=2))
        small = ctx.enter_context(tc.tile_pool(name="small", bufs=6))
        psum = ctx.enter_context(tc.psum_pool(name="psum", bufs=8))

        def bank(name):
            return psum.tile([P, BANK], F32, name=name, tag="bank")

        rows = const.tile([P, 2 * H + P], BF16, name="rows")
        nc.vector.memset(rows[:].bitcast(I32), 0)
        ones = const.tile([P, P], BF16, name="ones")
        nc.vector.memset(ones[:], 1.0)
        neg_half = const.tile([P, 1], F32, name="neg_half")
        nc.vector.memset(neg_half[:], -0.5)
        eps_col = const.tile([P, 1], F32, name="eps_col")
        nc.vector.memset(eps_col[:], EPS)
        ident = const.tile([P, P], F32, name="ident")
        make_identity(nc, ident[:])
        warm = const.tile([P, 1], F32, name="warm")
        nc.scalar.activation(out=warm[:], in_=neg_half[:], func=ACT.Silu)
        nc.scalar.dma_start(out=rows[0:1, 0:H], in_=g.unsqueeze(0))
        nc.scalar.dma_start(out=rows[0:1, H : 2 * H], in_=beta.unsqueeze(0))
        nc.scalar.dma_start(out=rows[0:NJ, 2 * H : 2 * H + P], in_=b1.rearrange("(j m) -> j m", m=P))

        w_raw = const.tile([P, 8, H], BF16, name="w_raw")
        for w in range(4):
            nc.sync.dma_start(
                out=w_raw[:, 2 * w : 2 * w + 2, :],
                in_=W1[256 * w : 256 * w + 256, :].rearrange("(p e) c -> p e c", e=2),
            )
        x_raw = []
        for c, n in enumerate(CHUNKS):
            xc = const.tile([P, n, D], BF16, name="x_raw%d" % c)
            nc.sync.dma_start(
                out=xc[:], in_=x[P * starts[c] : P * (starts[c] + n), :].rearrange("(p r) k -> p r k", r=n)
            )
            x_raw.append(xc)

        b1_rows = const.tile([P, P], F32, name="b1_rows")
        nc.vector.tensor_copy(out=b1_rows[:], in_=rows[:, 2 * H : 2 * H + P])
        b1_bank = bank("b1_bank")
        nc.tensor.transpose(b1_bank[:, 0:P], b1_rows[:], ident[:])
        b1_col = const.tile([P, NJ], F32, name="b1_col")
        nc.vector.tensor_copy(out=b1_col[:], in_=b1_bank[:, 0:NJ])

        w_grouped = const.tile([P, 2, H, 4], BF16, name="w_grouped", align_bytes=64)
        w_codes = const.tile([P, 2, H], U32, name="w_codes", align_bytes=64)
        w_scales = const.tile([P, 2, H], U8, name="w_scales", align_bytes=64)
        for gi in range(2):
            for lo in (0, BANK):
                cut = lo + W_VECTOR_COLS
                for copy, a, b in ((nc.vector.tensor_copy, lo, cut), (nc.scalar.copy, cut, lo + BANK)):
                    copy(
                        out=w_grouped[:, gi, a:b, :].rearrange("p (c i) t -> p c t i", i=4),
                        in_=w_raw[:, 4 * gi : 4 * gi + 4, a:b].rearrange("p t (c i) -> p c t i", i=4),
                    )
            for lo in (0, BANK):
                nc.vector.quantize_mx(
                    out=w_codes[:, gi, lo : lo + BANK].bitcast(FP8X4),
                    scales=w_scales[:, gi, lo : lo + BANK],
                    in_=w_grouped[:, gi, lo : lo + BANK, :].rearrange("p c t -> p (c t)"),
                )

        x_codes = {}
        x_scales = {}

        def prepare_x(c, copy):
            n = CHUNKS[c]
            nb = P * n
            grouped = work.tile([P, 8 * nb], BF16, name="x_grouped", tag="x_grouped", bufs=3, align_bytes=64)
            for r in range(n):
                turned = bank("x_turned")
                words = x_raw[c][:, r, :].bitcast(F32)
                for w in range(4):
                    nc.tensor.transpose(turned[:, P * w : P * w + P], words[:, P * w : P * w + P], ident[:])
                copy(
                    out=grouped[:].bitcast(F32).rearrange("p (g b u) -> p g b u", g=2, u=2)[:, :, P * r : P * r + P, :],
                    in_=turned[:].rearrange("p (g u b) -> p g b u", g=2, u=2),
                )
            x_codes[c] = const.tile([P, 2 * nb], U32, name="x_codes%d" % c, align_bytes=64)
            x_scales[c] = const.tile([P, 2 * nb], U8, name="x_scales%d" % c, align_bytes=64)
            nc.vector.quantize_mx(out=x_codes[c][:].bitcast(FP8X4), scales=x_scales[c][:], in_=grouped[:])

        hT = {}

        def produce(c, js):
            nb = P * CHUNKS[c]
            for j in js:
                if j == 0:
                    hT[c] = work.tile([P, NJ, nb], F32, name="hT", tag="hT", bufs=4)
                acc = bank("acc")
                for gi in range(2):
                    nc.tensor.matmul_mx(
                        out=acc[:, 0:nb],
                        lhsT=w_codes[:, gi, P * j : P * j + P].bitcast(FP8X4),
                        lhsT_scale=w_scales[:, gi, P * j : P * j + P],
                        rhs=x_codes[c][:, nb * gi : nb * gi + nb].bitcast(FP8X4),
                        rhs_scale=x_scales[c][:, nb * gi : nb * gi + nb],
                        start=(gi == 0),
                        stop=(gi == 1),
                    )
                nc.scalar.activation(
                    out=hT[c][:, j, :], in_=acc[:, 0:nb], func=ACT.Silu, bias=b1_col[:, j : j + 1], scale=1.0
                )

        gb = const.tile([P, 2 * H], F32, name="gb")

        def spread_g_beta():
            for q in range(4):
                spread = bank("spread")
                nc.tensor.matmul(
                    out=spread[:], lhsT=ones[:], rhs=rows[:, BANK * q : BANK * q + BANK], start=True, stop=True
                )
                nc.vector.tensor_copy(out=gb[:, BANK * q : BANK * q + BANK], in_=spread[:])

        junk = const.tile([P, H], F32, name="junk")
        centred = {}
        rstd = {}

        def centre(i):
            c = chunk_of[i]
            r = i - starts[c]
            halves = []
            for a in range(2):
                half = bank("h_half")
                for jj in range(4):
                    nc.tensor.transpose(half[:, P * jj : P * jj + P], hT[c][:, 4 * a + jj, P * r : P * r + P], ident[:])
                halves.append(half)
            t = work.tile([P, H], F32, name="centred", tag="centred", bufs=5)
            var_eps = small.tile([P, 1], F32, name="var_eps")
            if (i == 0 or i % 2 == 1) and i < VLIM:
                stats = small.tile([P, 2, 6], F32, name="stats")
                for a in range(2):
                    nc.vector.bn_stats(out=stats[:, a, :], in_=halves[a][:])
                mean_var = small.tile([P, 2], F32, name="mean_var")
                nc.vector.bn_aggr(out=mean_var[:], in_=stats[:].rearrange("p a s -> p (a s)"))
                nc.gpsimd.tensor_scalar(
                    out=var_eps[:], in0=mean_var[:, 1:2], scalar1=1.0, scalar2=EPS, op0=ALU.mult, op1=ALU.add
                )
                for a in range(2):
                    cols = slice(BANK * a, BANK * a + BANK)
                    nc.vector.scalar_tensor_tensor(
                        out=t[:, cols], in0=halves[a][:], scalar=mean_var[:, 0:1], in1=gb[:, cols],
                        op0=ALU.subtract, op1=ALU.mult,
                    )
            else:
                h = work.tile([P, H], F32, name="h", tag="h", bufs=4)
                sums = small.tile([P, 2], F32, name="sums")
                for a in range(2):
                    nc.scalar.activation(
                        out=h[:, BANK * a : BANK * a + BANK], in_=halves[a][:], func=ACT.Identity,
                        accum_out=sums[:, a : a + 1],
                    )
                neg_mean = small.tile([P, 1], F32, name="neg_mean")
                parts = small.tile([P, 2], F32, name="parts")
                nc.scalar.activation(out=parts[:], in_=sums[:], func=ACT.Identity, scale=-1.0 / H, accum_out=neg_mean[:])
                sum_sq = small.tile([P, 1], F32, name="sum_sq")
                nc.scalar.activation(out=junk[:], in_=h[:], func=ACT.Square, bias=neg_mean[:], accum_out=sum_sq[:])
                nc.scalar.activation(out=var_eps[:], in_=sum_sq[:], func=ACT.Identity, scale=1.0 / H, bias=eps_col[:])
                nc.vector.scalar_tensor_tensor(
                    out=t[:], in0=h[:], scalar=neg_mean[:], in1=gb[:, 0:H], op0=ALU.add, op1=ALU.mult
                )
            rstd[i] = small.tile([P, 1], F32, name="rstd")
            nc.gpsimd.tensor_tensor(out=rstd[i][:], in0=var_eps[:], in1=neg_half[:], op=ALU.pow)
            centred[i] = t

        def finish(i):
            c = chunk_of[i]
            n = CHUNKS[c]
            o = work.tile([P, H], F32, name="o", tag="o", bufs=4)
            if i % 2 == 0 and 2 <= i < 12:
                nc.gpsimd.tensor_scalar(
                    out=o[:], in0=centred[i][:], scalar1=rstd[i][:], scalar2=0.0, op0=ALU.mult, op1=ALU.add
                )
                nc.gpsimd.tensor_tensor(out=o[:], in0=o[:], in1=gb[:, H : 2 * H], op=ALU.add)
            else:
                nc.vector.scalar_tensor_tensor(
                    out=o[:], in0=centred[i][:], scalar=rstd[i][:], in1=gb[:, H : 2 * H], op0=ALU.mult, op1=ALU.add
                )
            rows_c = out[P * starts[c] : P * (starts[c] + n), :].rearrange("(p r) h -> p r h", r=n)
            nc.sync.dma_start(out=rows_c[:, i - starts[c], :], in_=o[:])

        prepare_x(0, nc.scalar.copy)
        prepare_x(1, nc.scalar.copy)
        prepare_x(2, nc.vector.tensor_copy)
        produce(0, range(NJ))
        spread_g_beta()
        produce(1, range(NJ))
        for i in range(NT):
            c = chunk_of[i]
            n = CHUNKS[c]
            r = i - starts[c]
            if r == 0 and c + 3 < len(CHUNKS):
                prepare_x(c + 3, nc.vector.tensor_copy if c + 3 in XV else nc.scalar.copy)
            if c + 2 < len(CHUNKS):
                produce(c + 2, range(NJ * r // n, NJ * (r + 1) // n))
            centre(i)
            if i >= 2:
                finish(i - 2)
        finish(NT - 2)
        finish(NT - 1)
